import numpy as np
import ml_dtypes


def mxq(x, axis, fmt="e4m3"):
    dtype, down = {"e4m3": (ml_dtypes.float8_e4m3fn, 7), "e5m2": (ml_dtypes.float8_e5m2, 14)}[fmt]
    v = np.moveaxis(np.asarray(x, np.float32).astype(ml_dtypes.bfloat16).astype(np.float64), axis, -1)
    blocks = v.reshape(v.shape[:-1] + (-1, 32))
    amax = np.abs(blocks).max(-1, keepdims=True)
    byte = np.maximum(np.where(amax > 0, np.frexp(amax)[1] - 1 + 127, 0) - down, 1)
    scale = np.exp2(byte - 127.0)
    codes = (blocks / scale).astype(np.float32).astype(dtype).astype(np.float64)
    return np.moveaxis((codes * scale).reshape(v.shape), -1, axis)


WIDE = False


def mx_kscale(k):
    if not WIDE:
        return np.ones(k)
    levels = np.array([10, -10, 5, -5, 0])
    a = np.random.permutation(np.resize(levels, k // 512 * 4)).reshape(k // 512, 4)
    idx = np.arange(k)
    return np.exp2(a[idx // 512, idx % 128 // 32])


BF16 = ml_dtypes.bfloat16


def bf(x):
    return np.asarray(x, np.float32).astype(BF16)


def f64(x):
    return np.asarray(x).astype(np.float64)


E2M1 = np.array([0.0, 0.5, 1.0, 1.5, 2.0, 3.0, 4.0, 6.0, -0.0, -0.5, -1.0, -1.5, -2.0, -3.0, -4.0, -6.0])


def pack_weight(w, fmt):
    k, n = w.shape
    w = f64(bf(w)).reshape(k // 32, 32, n)
    amax = np.abs(w).max(1)
    if fmt == "e4m3":
        byte = np.frexp(amax)[1] - 1 + 127 - 7
    else:
        mant, ex = np.frexp(amax / 6.0)
        byte = np.where(mant > 0.5, ex, ex - 1) + 127
    byte = np.clip(np.where(amax > 0, byte, 1), 1, 254)
    scaled = (w * np.exp2(127.0 - byte)[:, None, :]).reshape(k, n).astype(np.float32)
    by_word = np.ascontiguousarray(scaled.reshape(k // 512, 128, 4, n).transpose(0, 1, 3, 2))
    if fmt == "e4m3":
        words = by_word.astype(ml_dtypes.float8_e4m3fn).view(np.uint8)
    else:
        c = by_word.astype(ml_dtypes.float4_e2m1fn).view(np.uint8) & 0xF
        words = c[..., 0::2] | (c[..., 1::2] << 4)
    return np.ascontiguousarray(words), np.ascontiguousarray(byte.astype(np.uint8).reshape(k // 512, 16, n))


def unpack_weight(words, scales, fmt):
    g, p, n, _ = words.shape
    if fmt == "e4m3":
        vals = np.ascontiguousarray(words).view(ml_dtypes.float8_e4m3fn).astype(np.float64)
    else:
        nib = np.empty((g, p, n, 4), np.uint8)
        nib[..., 0::2] = words & 0xF
        nib[..., 1::2] = words >> 4
        vals = E2M1[nib]
    vals = vals * np.repeat(np.exp2(scales.astype(np.float64) - 127.0), 8, axis=1)[..., None]
    return vals.transpose(0, 1, 3, 2).reshape(g * 512, n)

def pack4(w):
    words, scales = pack_weight(w, "e2m1")
    return words.reshape(words.shape[0], 128, -1), scales


def unpack4(words, scales):
    return unpack_weight(words.reshape(words.shape[0], 128, -1, 2), scales, "e2m1")


B, S, C, HD = 1, 512, 3072, 128
H = C // HD
HP = HD // 2
EPS = 1e-6
THETA = 10000.0


def rmsnorm(h, g):
    return h * (1.0 / np.sqrt(np.mean(h * h, axis=-1, keepdims=True) + EPS)) * g


def apply_rope1(h, freqs):
    sh = h.shape
    h_ = h.reshape(*sh[:-1], -1, 1, 2)
    out = freqs[..., 0] * h_[..., 0] + freqs[..., 1] * h_[..., 1]
    return out.reshape(sh)


def setup_inputs():
    s = mx_kscale(C)
    pos = f64(np.random.randint(0, S, size=(S, 1)))
    inv_freq = 1.0 / THETA ** (np.arange(HP) / HP)
    ang = pos * inv_freq
    cos, sin = np.cos(ang), np.sin(ang)
    rot = np.stack([np.stack([cos, -sin], -1), np.stack([sin, cos], -1)], -2)
    x = bf(np.random.standard_normal((B, S, C)) * s)
    w = np.random.standard_normal((C, C)) / np.sqrt(C) / s[None, :]
    w_words, w_scales = pack4(np.ascontiguousarray(w.T))
    return {"x": x,
            "freqs": bf(rot[None, :, None]),
            "w_words": w_words,
            "w_scales": w_scales,
            "b": bf(np.random.standard_normal(C) * 0.3),
            "g": bf(1.0 + 0.1 * np.random.standard_normal(HD))}


def reference(x, freqs, w_words, w_scales, b, g):
    p = (mxq(f64(x), 2, "e4m3") @ unpack4(w_words, w_scales)) + f64(b)
    h = p.reshape(B, S, H, HD)
    return apply_rope1(rmsnorm(h, f64(g)), f64(freqs))

@@ -1,0 +1,223 @@
+from contextlib import ExitStack
+
+import concourse.mybir as mybir
+from concourse.masks import make_identity
+
+F32 = mybir.dt.float32
+BF16 = mybir.dt.bfloat16
+I32 = mybir.dt.int32
+U32 = mybir.dt.uint32
+U8 = mybir.dt.uint8
+FP8X4 = mybir.dt.float8_e4m3fn_x4
+FP4X4 = mybir.dt.float4_e2m1fn_x4
+ACT = mybir.ActivationFunctionType
+ALU = mybir.AluOpType
+
+P = 128
+TOKENS = 512
+FEATURES = 3072
+HEAD = 128
+PAIRS = HEAD // 2
+EPS = 1e-6
+
+K_PASS = 4 * P
+PASSES = FEATURES // K_PASS
+WORDS_PASS = K_PASS // 2
+N_BLOCK = 512
+BLOCK_HEADS = N_BLOCK // HEAD
+N_BLOCKS = FEATURES // N_BLOCK
+TOKEN_TILES = TOKENS // P
+BANKS = N_BLOCKS * TOKEN_TILES
+PLANE_BLOCKS = 2
+AHEAD = 2
+
+FLOPS = 2 * TOKENS * FEATURES * FEATURES
+
+
+def tile_selfattention_pa_kernel(tc, x, freqs, w_words, w_scales, b, g, out):
+    nc = tc.nc
+
+    x_tiles = x.flatten_outer_dims().rearrange("(t p) k -> t p k", p=P)
+    out_tiles = out.flatten_outer_dims().rearrange("(t p h) d -> t p (h d)", p=P, h=FEATURES // HEAD)
+    freqs_rows = freqs.flatten_outer_dims().rearrange("(t p j i) c -> p t (j i c)", p=P, j=PAIRS, i=2)
+    w_words_i32 = w_words.bitcast(I32)
+    w_scales_i32 = w_scales.bitcast(I32)
+
+    with ExitStack() as ctx:
+        keep = ctx.enter_context(tc.tile_pool(name="keep", bufs=1))
+        stage = ctx.enter_context(tc.tile_pool(name="stage", bufs=4))
+        table_banks = ctx.enter_context(tc.psum_pool(name="table_banks", bufs=1))
+        turned_banks = ctx.enter_context(tc.psum_pool(name="turned_banks", bufs=3))
+        product_banks = ctx.enter_context(tc.psum_pool(name="product_banks", bufs=3))
+        ctx.enter_context(tc.manual_schedule())
+
+        x_raw = [keep.tile([P, FEATURES], BF16, name="x_raw%d" % t) for t in range(TOKEN_TILES)]
+        x_codes = [
+            keep.tile([P, PASSES, P], U32, name="x_codes%d" % t, align_bytes=64) for t in range(TOKEN_TILES)
+        ]
+        x_planes = [
+            keep.tile([P, PASSES, P], U8, name="x_planes%d" % t, align_bytes=64) for t in range(TOKEN_TILES)
+        ]
+        w_codes = [
+            keep.tile([P, PASSES, 2 * N_BLOCK], U8, name="w_codes%d" % j, align_bytes=64) for j in range(N_BLOCKS)
+        ]
+        w_planes = [
+            keep.tile([P, PASSES, PLANE_BLOCKS * N_BLOCK], U8, name="w_planes%d" % s, align_bytes=64)
+            for s in range(N_BLOCKS // PLANE_BLOCKS)
+        ]
+        bias = [keep.tile([P, N_BLOCK], BF16, name="bias%d" % j) for j in range(N_BLOCKS)]
+        freqs_sb = keep.tile([P, TOKEN_TILES, 4 * PAIRS], BF16)
+        gain = keep.tile([P, HEAD], BF16)
+        tables_sb = keep.tile([P, TOKEN_TILES, 2, PAIRS, 2], F32)
+        identity = keep.tile([P, P], F32)
+        eps = keep.tile([P, 1], F32)
+        warm = keep.tile([P, 1], F32)
+        tables = [table_banks.tile([P, 2, 4 * PAIRS], F32, name="tables%d" % s) for s in range(TOKEN_TILES // 2)]
+
+        def load_tokens(t):
+            nc.sync.dma_start(out=x_raw[t][:], in_=x_tiles[t])
+
+        def load_features(j):
+            if j % PLANE_BLOCKS == 0:
+                s = j // PLANE_BLOCKS
+                words = PLANE_BLOCKS * N_BLOCK // 4
+                for r in range(4):
+                    nc.sync.dma_start(
+                        out=w_planes[s][r:P:32, :, :].bitcast(I32),
+                        in_=w_scales_i32[:, r:16:4, s * words : (s + 1) * words].rearrange("c q w -> q c w"),
+                    )
+            words = 2 * N_BLOCK // 4
+            nc.sync.dma_start(
+                out=w_codes[j][:].bitcast(I32),
+                in_=w_words_i32[:, :, j * words : (j + 1) * words].rearrange("c p w -> p c w"),
+            )
+            nc.sync.dma_start(out=bias[j][:], in_=b[j * N_BLOCK : (j + 1) * N_BLOCK].partition_broadcast(P))
+
+        def prepare_tokens(t):
+            words = x_raw[t][:].bitcast(F32)
+            for half in range(PASSES // 2):
+                turned = turned_banks.tile([P, 2, 2, P], F32)
+                for a in range(2):
+                    first = (2 * half + a) * WORDS_PASS
+                    for u in range(2):
+                        nc.tensor.transpose(
+                            turned[:, a, u, :], words[:, first + u : first + WORDS_PASS : 2], identity[:]
+                        )
+                grouped = stage.tile([P, 2 * K_PASS], BF16, align_bytes=64)
+                nc.scalar.copy(
+                    out=grouped[:].bitcast(F32).rearrange("p (a r u) -> p a r u", a=2, u=2),
+                    in_=turned[:].rearrange("p a u r -> p a r u"),
+                )
+                passes = slice(2 * half, 2 * half + 2)
+                nc.vector.quantize_mx(
+                    out=x_codes[t][:, passes, :].rearrange("p a r -> p (a r)").bitcast(FP8X4),
+                    scales=x_planes[t][:, passes, :].rearrange("p a r -> p (a r)"),
+                    in_=grouped[:],
+                )
+
+        def build_tables():
+            for t in range(TOKEN_TILES):
+                nc.gpsimd.tensor_tensor(
+                    out=tables_sb[:, t],
+                    in0=freqs_sb[:, t, :].rearrange("p (j i c) -> p c j i", i=2, c=2),
+                    in1=gain[:].rearrange("p (j c) -> p c j", c=2).unsqueeze(3).to_broadcast([P, 2, PAIRS, 2]),
+                    op=ALU.mult,
+                )
+                nc.tensor.matmul(
+                    out=tables[t // 2][:, t % 2, :],
+                    lhsT=identity[:],
+                    rhs=tables_sb[:, t].rearrange("p c j i -> p (c j i)"),
+                    start=True,
+                    stop=True,
+                )
+
+        def project(j, t):
+            bank = product_banks.tile([P, N_BLOCK], F32)
+            plane = w_planes[j // PLANE_BLOCKS]
+            cols = slice((j % PLANE_BLOCKS) * N_BLOCK, (j % PLANE_BLOCKS + 1) * N_BLOCK)
+            for c in range(PASSES):
+                nc.tensor.matmul_mx(
+                    out=bank[:],
+                    lhsT=x_codes[t][:, c, :].bitcast(FP8X4),
+                    lhsT_scale=x_planes[t][:, c, :],
+                    rhs=w_codes[j][:, c, :].bitcast(FP4X4),
+                    rhs_scale=plane[:, c, cols],
+                    start=(c == 0),
+                    stop=(c == PASSES - 1),
+                )
+            return bank
+
+        def norm_and_rotate(j, t, bank):
+            u = stage.tile([P, N_BLOCK], F32)
+            nc.vector.tensor_tensor(out=u[:], in0=bank[:], in1=bias[j][:], op=ALU.add)
+
+            sums = stage.tile([P, BLOCK_HEADS], F32)
+            for h in range(BLOCK_HEADS):
+                squares = stage.tile([P, HEAD], F32)
+                nc.scalar.activation(
+                    out=squares[:], in_=u[:, h * HEAD : (h + 1) * HEAD], func=ACT.Square, accum_out=sums[:, h : h + 1]
+                )
+
+            shape = [P, BLOCK_HEADS, PAIRS, 2]
+            table = tables[t // 2][:, t % 2, :].rearrange("p (c j i) -> p c j i", c=2, i=2)
+            u_pairs = u[:].rearrange("p (h j c) -> p h j c", h=BLOCK_HEADS, c=2)
+            products = []
+            for c in range(2):
+                product = stage.tile([P, N_BLOCK], F32, name="product%d" % c)
+                nc.vector.tensor_tensor(
+                    out=product[:].rearrange("p (h j i) -> p h j i", h=BLOCK_HEADS, i=2),
+                    in0=u_pairs[:, :, :, c : c + 1].to_broadcast(shape),
+                    in1=table[:, c].unsqueeze(1).to_broadcast(shape),
+                    op=ALU.mult,
+                )
+                products.append(product)
+
+            inv_rms = stage.tile([P, BLOCK_HEADS], F32)
+            nc.scalar.activation(
+                out=inv_rms[:], in_=sums[:], func=ACT.Abs_reciprocal_sqrt, bias=eps[:], scale=1.0 / HEAD
+            )
+
+            rotated = stage.tile([P, N_BLOCK], F32)
+            nc.gpsimd.tensor_tensor(out=rotated[:], in0=products[0][:], in1=products[1][:], op=ALU.add)
+            return rotated, inv_rms
+
+        def scale_and_store(j, t, rotated, inv_rms):
+            result = stage.tile([P, N_BLOCK], F32)
+            for h in range(BLOCK_HEADS):
+                head = slice(h * HEAD, (h + 1) * HEAD)
+                nc.scalar.activation(
+                    out=result[:, head], in_=rotated[:, head], func=ACT.Copy, scale=inv_rms[:, h : h + 1]
+                )
+            nc.sync.dma_start(out=out_tiles[t][:, j * N_BLOCK : (j + 1) * N_BLOCK], in_=result[:])
+
+        nc.vector.memset(eps[:], EPS)
+        for plane in w_planes:
+            nc.vector.memset(plane[:].bitcast(I32), 0)
+        make_identity(nc, identity[:])
+        nc.scalar.activation(out=warm[:], in_=eps[:], func=ACT.Abs_reciprocal_sqrt)
+
+        nc.scalar.dma_start(out=gain[:], in_=g.partition_broadcast(P))
+        nc.scalar.dma_start(out=freqs_sb[:], in_=freqs_rows)
+        for t in range(AHEAD):
+            load_tokens(t)
+        load_features(0)
+        for t in range(AHEAD, TOKEN_TILES):
+            load_tokens(t)
+        for j in range(1, N_BLOCKS):
+            load_features(j)
+
+        for t in range(AHEAD):
+            prepare_tokens(t)
+        build_tables()
+
+        waiting = None
+        for j in range(N_BLOCKS):
+            for t in range(TOKEN_TILES):
+                bank = project(j, t)
+                rotated, inv_rms = norm_and_rotate(j, t, bank)
+                if waiting is not None:
+                    scale_and_store(*waiting)
+                waiting = (j, t, rotated, inv_rms)
+                if j == 0 and t + AHEAD < TOKEN_TILES:
+                    prepare_tokens(t + AHEAD)
+        scale_and_store(*waiting)

@@ -22,7 +22,6 @@ EPS = 1e-6
 
 K_PASS = 4 * P
 PASSES = FEATURES // K_PASS
-WORDS_PASS = K_PASS // 2
 N_BLOCK = 512
 BLOCK_HEADS = N_BLOCK // HEAD
 N_BLOCKS = FEATURES // N_BLOCK
@@ -52,6 +51,7 @@ def tile_selfattention_pa_kernel(tc, x, freqs, w_words, w_scales, b, g, out):
         ctx.enter_context(tc.manual_schedule())
 
         x_raw = [keep.tile([P, FEATURES], BF16, name="x_raw%d" % t) for t in range(TOKEN_TILES)]
+        x_sorted = [keep.tile([P, PASSES, 2, P], F32, name="x_sorted%d" % t) for t in range(TOKEN_TILES)]
         x_codes = [
             keep.tile([P, PASSES, P], U32, name="x_codes%d" % t, align_bytes=64) for t in range(TOKEN_TILES)
         ]
@@ -65,11 +65,12 @@ def tile_selfattention_pa_kernel(tc, x, freqs, w_words, w_scales, b, g, out):
             keep.tile([P, PASSES, PLANE_BLOCKS * N_BLOCK], U8, name="w_planes%d" % s, align_bytes=64)
             for s in range(N_BLOCKS // PLANE_BLOCKS)
         ]
-        bias = [keep.tile([P, N_BLOCK], BF16, name="bias%d" % j) for j in range(N_BLOCKS)]
+        vectors = keep.tile([P, N_BLOCK], BF16)
+        bias = [keep.tile([P, N_BLOCK], F32, name="bias%d" % j) for j in range(N_BLOCKS)]
         freqs_sb = keep.tile([P, TOKEN_TILES, 4 * PAIRS], BF16)
-        gain = keep.tile([P, HEAD], BF16)
         tables_sb = keep.tile([P, TOKEN_TILES, 2, PAIRS, 2], F32)
         identity = keep.tile([P, P], F32)
+        identity_bf = keep.tile([P, P], BF16)
         eps = keep.tile([P, 1], F32)
         warm = keep.tile([P, 1], F32)
         tables = [table_banks.tile([P, 2, 4 * PAIRS], F32, name="tables%d" % s) for s in range(TOKEN_TILES // 2)]
@@ -91,47 +92,44 @@ def tile_selfattention_pa_kernel(tc, x, freqs, w_words, w_scales, b, g, out):
                 out=w_codes[j][:].bitcast(I32),
                 in_=w_words_i32[:, :, j * words : (j + 1) * words].rearrange("c p w -> p c w"),
             )
-            nc.sync.dma_start(out=bias[j][:], in_=b[j * N_BLOCK : (j + 1) * N_BLOCK].partition_broadcast(P))
 
-        def prepare_tokens(t):
-            words = x_raw[t][:].bitcast(F32)
+        def spread(row):
+            bank = product_banks.tile([P, N_BLOCK], F32)
+            nc.tensor.matmul(
+                out=bank[:],
+                lhsT=identity_bf[:, row : row + 1].to_broadcast([P, P]),
+                rhs=vectors[:],
+                start=True,
+                stop=True,
+            )
+            return bank
+
+        def sort_words(t):
+            words = x_raw[t][:].bitcast(F32).rearrange("p (c r u) -> p c u r", r=P, u=2)
             for half in range(PASSES // 2):
+                passes = slice(2 * half, 2 * half + 2)
+                nc.vector.tensor_copy(out=x_sorted[t][:, passes], in_=words[:, passes])
+
+        def transpose_and_quantise(t):
+            for half in range(PASSES // 2):
+                passes = slice(2 * half, 2 * half + 2)
                 turned = turned_banks.tile([P, 2, 2, P], F32)
                 for a in range(2):
-                    first = (2 * half + a) * WORDS_PASS
                     for u in range(2):
-                        nc.tensor.transpose(
-                            turned[:, a, u, :], words[:, first + u : first + WORDS_PASS : 2], identity[:]
-                        )
+                        nc.tensor.transpose(turned[:, a, u, :], x_sorted[t][:, 2 * half + a, u, :], identity[:])
                 grouped = stage.tile([P, 2 * K_PASS], BF16, align_bytes=64)
                 nc.scalar.copy(
                     out=grouped[:].bitcast(F32).rearrange("p (a r u) -> p a r u", a=2, u=2),
                     in_=turned[:].rearrange("p a u r -> p a r u"),
                 )
-                passes = slice(2 * half, 2 * half + 2)
                 nc.vector.quantize_mx(
                     out=x_codes[t][:, passes, :].rearrange("p a r -> p (a r)").bitcast(FP8X4),
                     scales=x_planes[t][:, passes, :].rearrange("p a r -> p (a r)"),
                     in_=grouped[:],
                 )
 
-        def build_tables():
-            for t in range(TOKEN_TILES):
-                nc.gpsimd.tensor_tensor(
-                    out=tables_sb[:, t],
-                    in0=freqs_sb[:, t, :].rearrange("p (j i c) -> p c j i", i=2, c=2),
-                    in1=gain[:].rearrange("p (j c) -> p c j", c=2).unsqueeze(3).to_broadcast([P, 2, PAIRS, 2]),
-                    op=ALU.mult,
-                )
-                nc.tensor.matmul(
-                    out=tables[t // 2][:, t % 2, :],
-                    lhsT=identity[:],
-                    rhs=tables_sb[:, t].rearrange("p c j i -> p (c j i)"),
-                    start=True,
-                    stop=True,
-                )
-
-        def project(j, t):
+        def project(k):
+            j, t = divmod(k, TOKEN_TILES)
             bank = product_banks.tile([P, N_BLOCK], F32)
             plane = w_planes[j // PLANE_BLOCKS]
             cols = slice((j % PLANE_BLOCKS) * N_BLOCK, (j % PLANE_BLOCKS + 1) * N_BLOCK)
@@ -147,56 +145,69 @@ def tile_selfattention_pa_kernel(tc, x, freqs, w_words, w_scales, b, g, out):
                 )
             return bank
 
-        def norm_and_rotate(j, t, bank):
-            u = stage.tile([P, N_BLOCK], F32)
-            nc.vector.tensor_tensor(out=u[:], in0=bank[:], in1=bias[j][:], op=ALU.add)
+        biased = {}
+        products = {}
+        rotated = {}
+        inv_rms = {}
 
+        def add_bias(k, bank):
+            biased[k] = stage.tile([P, N_BLOCK], F32, name="biased")
+            nc.vector.tensor_tensor(out=biased[k][:], in0=bank[:], in1=bias[k // TOKEN_TILES][:], op=ALU.add)
+
+        def multiply_table(k, c):
+            t = k % TOKEN_TILES
+            shape = [P, BLOCK_HEADS, PAIRS, 2]
+            table = tables[t // 2][:, t % 2, :].rearrange("p (c j i) -> p c j i", c=2, i=2)
+            pairs = biased[k][:].rearrange("p (h j c) -> p h j c", h=BLOCK_HEADS, c=2)
+            products[k, c] = stage.tile([P, N_BLOCK], F32, name="product%d" % c)
+            nc.vector.tensor_tensor(
+                out=products[k, c][:].rearrange("p (h j i) -> p h j i", h=BLOCK_HEADS, i=2),
+                in0=pairs[:, :, :, c : c + 1].to_broadcast(shape),
+                in1=table[:, c].unsqueeze(1).to_broadcast(shape),
+                op=ALU.mult,
+            )
+
+        def add_products(k):
+            rotated[k] = stage.tile([P, N_BLOCK], F32, name="rotated")
+            nc.gpsimd.tensor_tensor(out=rotated[k][:], in0=products[k, 0][:], in1=products[k, 1][:], op=ALU.add)
+
+        def sum_squares(k):
             sums = stage.tile([P, BLOCK_HEADS], F32)
             for h in range(BLOCK_HEADS):
                 squares = stage.tile([P, HEAD], F32)
                 nc.scalar.activation(
-                    out=squares[:], in_=u[:, h * HEAD : (h + 1) * HEAD], func=ACT.Square, accum_out=sums[:, h : h + 1]
+                    out=squares[:],
+                    in_=biased[k][:, h * HEAD : (h + 1) * HEAD],
+                    func=ACT.Square,
+                    accum_out=sums[:, h : h + 1],
                 )
+            return sums
 
-            shape = [P, BLOCK_HEADS, PAIRS, 2]
-            table = tables[t // 2][:, t % 2, :].rearrange("p (c j i) -> p c j i", c=2, i=2)
-            u_pairs = u[:].rearrange("p (h j c) -> p h j c", h=BLOCK_HEADS, c=2)
-            products = []
-            for c in range(2):
-                product = stage.tile([P, N_BLOCK], F32, name="product%d" % c)
-                nc.vector.tensor_tensor(
-                    out=product[:].rearrange("p (h j i) -> p h j i", h=BLOCK_HEADS, i=2),
-                    in0=u_pairs[:, :, :, c : c + 1].to_broadcast(shape),
-                    in1=table[:, c].unsqueeze(1).to_broadcast(shape),
-                    op=ALU.mult,
-                )
-                products.append(product)
-
-            inv_rms = stage.tile([P, BLOCK_HEADS], F32)
+        def invert_rms(k, sums):
+            inv_rms[k] = stage.tile([P, BLOCK_HEADS], F32, name="inv_rms")
             nc.scalar.activation(
-                out=inv_rms[:], in_=sums[:], func=ACT.Abs_reciprocal_sqrt, bias=eps[:], scale=1.0 / HEAD
+                out=inv_rms[k][:], in_=sums[:], func=ACT.Abs_reciprocal_sqrt, bias=eps[:], scale=1.0 / HEAD
             )
 
-            rotated = stage.tile([P, N_BLOCK], F32)
-            nc.gpsimd.tensor_tensor(out=rotated[:], in0=products[0][:], in1=products[1][:], op=ALU.add)
-            return rotated, inv_rms
-
-        def scale_and_store(j, t, rotated, inv_rms):
+        def scale_and_store(k):
+            j, t = divmod(k, TOKEN_TILES)
             result = stage.tile([P, N_BLOCK], F32)
             for h in range(BLOCK_HEADS):
                 head = slice(h * HEAD, (h + 1) * HEAD)
                 nc.scalar.activation(
-                    out=result[:, head], in_=rotated[:, head], func=ACT.Copy, scale=inv_rms[:, h : h + 1]
+                    out=result[:, head], in_=rotated[k][:, head], func=ACT.Copy, scale=inv_rms[k][:, h : h + 1]
                 )
             nc.sync.dma_start(out=out_tiles[t][:, j * N_BLOCK : (j + 1) * N_BLOCK], in_=result[:])
 
+        nc.vector.memset(vectors[:], 0.0)
         nc.vector.memset(eps[:], EPS)
         for plane in w_planes:
             nc.vector.memset(plane[:].bitcast(I32), 0)
+        make_identity(nc, identity_bf[:])
         make_identity(nc, identity[:])
-        nc.scalar.activation(out=warm[:], in_=eps[:], func=ACT.Abs_reciprocal_sqrt)
 
-        nc.scalar.dma_start(out=gain[:], in_=g.partition_broadcast(P))
+        nc.scalar.dma_start(out=vectors[0:N_BLOCKS, :], in_=b.rearrange("(r n) -> r n", n=N_BLOCK))
+        nc.scalar.dma_start(out=vectors[N_BLOCKS : N_BLOCKS + 1, 0:HEAD], in_=g.rearrange("(r n) -> r n", n=HEAD))
         nc.scalar.dma_start(out=freqs_sb[:], in_=freqs_rows)
         for t in range(AHEAD):
             load_tokens(t)
@@ -206,18 +217,49 @@ def tile_selfattention_pa_kernel(tc, x, freqs, w_words, w_scales, b, g, out):
         for j in range(1, N_BLOCKS):
             load_features(j)
 
-        for t in range(AHEAD):
-            prepare_tokens(t)
-        build_tables()
+        nc.scalar.activation(out=warm[:], in_=eps[:], func=ACT.Abs_reciprocal_sqrt)
 
-        waiting = None
+        gain_bank = spread(N_BLOCKS)
         for j in range(N_BLOCKS):
-            for t in range(TOKEN_TILES):
-                bank = project(j, t)
-                rotated, inv_rms = norm_and_rotate(j, t, bank)
-                if waiting is not None:
-                    scale_and_store(*waiting)
-                waiting = (j, t, rotated, inv_rms)
-                if j == 0 and t + AHEAD < TOKEN_TILES:
-                    prepare_tokens(t + AHEAD)
-        scale_and_store(*waiting)
+            nc.scalar.copy(out=bias[j][:], in_=spread(j)[:])
+
+        sort_words(0)
+        gain = gain_bank[:, 0:HEAD].rearrange("p (j c) -> p c j", c=2).unsqueeze(3).to_broadcast([P, 2, PAIRS, 2])
+        for t in range(TOKEN_TILES):
+            nc.vector.tensor_tensor(
+                out=tables_sb[:, t],
+                in0=freqs_sb[:, t, :].rearrange("p (j i c) -> p c j i", i=2, c=2),
+                in1=gain,
+                op=ALU.mult,
+            )
+        sort_words(1)
+        transpose_and_quantise(0)
+        for t in range(TOKEN_TILES):
+            nc.tensor.matmul(
+                out=tables[t // 2][:, t % 2, :],
+                lhsT=identity[:],
+                rhs=tables_sb[:, t].rearrange("p c j i -> p (c j i)"),
+                start=True,
+                stop=True,
+            )
+        transpose_and_quantise(1)
+
+        for k in range(BANKS + 2):
+            prepare = k + AHEAD < TOKEN_TILES
+            if k < BANKS:
+                bank = project(k)
+                if prepare:
+                    sort_words(k + AHEAD)
+                add_bias(k, bank)
+            if 1 <= k <= BANKS:
+                multiply_table(k - 1, 1)
+                add_products(k - 1)
+            if k < BANKS:
+                multiply_table(k, 0)
+                sums = sum_squares(k)
+            if k >= 2:
+                scale_and_store(k - 2)
+            if k < BANKS:
+                invert_rms(k, sums)
+                if prepare:
+                    transpose_and_quantise(k + AHEAD)

@@ -28,7 +28,6 @@ N_BLOCKS = FEATURES // N_BLOCK
 TOKEN_TILES = TOKENS // P
 BANKS = N_BLOCKS * TOKEN_TILES
 PLANE_BLOCKS = 2
-AHEAD = 2
 
 FLOPS = 2 * TOKENS * FEATURES * FEATURES
 
@@ -45,9 +44,9 @@ def tile_selfattention_pa_kernel(tc, x, freqs, w_words, w_scales, b, g, out):
     with ExitStack() as ctx:
         keep = ctx.enter_context(tc.tile_pool(name="keep", bufs=1))
         stage = ctx.enter_context(tc.tile_pool(name="stage", bufs=4))
+        results = ctx.enter_context(tc.tile_pool(name="results", bufs=8))
         table_banks = ctx.enter_context(tc.psum_pool(name="table_banks", bufs=1))
-        turned_banks = ctx.enter_context(tc.psum_pool(name="turned_banks", bufs=3))
-        product_banks = ctx.enter_context(tc.psum_pool(name="product_banks", bufs=3))
+        banks = ctx.enter_context(tc.psum_pool(name="banks", bufs=5))
         ctx.enter_context(tc.manual_schedule())
 
         x_raw = [keep.tile([P, FEATURES], BF16, name="x_raw%d" % t) for t in range(TOKEN_TILES)]
@@ -74,6 +73,7 @@ def tile_selfattention_pa_kernel(tc, x, freqs, w_words, w_scales, b, g, out):
         eps = keep.tile([P, 1], F32)
         warm = keep.tile([P, 1], F32)
         tables = [table_banks.tile([P, 2, 4 * PAIRS], F32, name="tables%d" % s) for s in range(TOKEN_TILES // 2)]
+        gain_bank = table_banks.tile([P, N_BLOCK], F32)
 
         def load_tokens(t):
             nc.sync.dma_start(out=x_raw[t][:], in_=x_tiles[t])
@@ -93,8 +93,7 @@ def tile_selfattention_pa_kernel(tc, x, freqs, w_words, w_scales, b, g, out):
                 in_=w_words_i32[:, :, j * words : (j + 1) * words].rearrange("c p w -> p c w"),
             )
 
-        def spread(row):
-            bank = product_banks.tile([P, N_BLOCK], F32)
+        def spread(row, bank):
             nc.tensor.matmul(
                 out=bank[:],
                 lhsT=identity_bf[:, row : row + 1].to_broadcast([P, P]),
@@ -102,35 +101,41 @@ def tile_selfattention_pa_kernel(tc, x, freqs, w_words, w_scales, b, g, out):
                 start=True,
                 stop=True,
             )
-            return bank
 
-        def sort_words(t):
+        def spread_bias(j):
+            bank = banks.tile([P, N_BLOCK], F32, tag="bank")
+            spread(j, bank)
+            nc.scalar.copy(out=bias[j][:], in_=bank[:])
+
+        grouped = {}
+
+        def transpose(t):
             words = x_raw[t][:].bitcast(F32).rearrange("p (c r u) -> p c u r", r=P, u=2)
             for half in range(PASSES // 2):
                 passes = slice(2 * half, 2 * half + 2)
                 nc.vector.tensor_copy(out=x_sorted[t][:, passes], in_=words[:, passes])
-
-        def transpose_and_quantise(t):
-            for half in range(PASSES // 2):
-                passes = slice(2 * half, 2 * half + 2)
-                turned = turned_banks.tile([P, 2, 2, P], F32)
+                turned = banks.tile([P, 2, 2, P], F32, tag="bank")
                 for a in range(2):
                     for u in range(2):
                         nc.tensor.transpose(turned[:, a, u, :], x_sorted[t][:, 2 * half + a, u, :], identity[:])
-                grouped = stage.tile([P, 2 * K_PASS], BF16, align_bytes=64)
+                grouped[t, half] = stage.tile([P, 2 * K_PASS], BF16, name="grouped", bufs=TOKEN_TILES * PASSES // 2, align_bytes=64)
                 nc.scalar.copy(
-                    out=grouped[:].bitcast(F32).rearrange("p (a r u) -> p a r u", a=2, u=2),
+                    out=grouped[t, half][:].bitcast(F32).rearrange("p (a r u) -> p a r u", a=2, u=2),
                     in_=turned[:].rearrange("p a u r -> p a r u"),
                 )
+
+        def quantise(t):
+            for half in range(PASSES // 2):
+                passes = slice(2 * half, 2 * half + 2)
                 nc.vector.quantize_mx(
                     out=x_codes[t][:, passes, :].rearrange("p a r -> p (a r)").bitcast(FP8X4),
                     scales=x_planes[t][:, passes, :].rearrange("p a r -> p (a r)"),
-                    in_=grouped[:],
+                    in_=grouped[t, half][:],
                 )
 
         def project(k):
             j, t = divmod(k, TOKEN_TILES)
-            bank = product_banks.tile([P, N_BLOCK], F32)
+            bank = banks.tile([P, N_BLOCK], F32, tag="bank")
             plane = w_planes[j // PLANE_BLOCKS]
             cols = slice((j % PLANE_BLOCKS) * N_BLOCK, (j % PLANE_BLOCKS + 1) * N_BLOCK)
             for c in range(PASSES):
@@ -169,7 +174,8 @@ def tile_selfattention_pa_kernel(tc, x, freqs, w_words, w_scales, b, g, out):
 
         def add_products(k):
             rotated[k] = stage.tile([P, N_BLOCK], F32, name="rotated")
-            nc.gpsimd.tensor_tensor(out=rotated[k][:], in0=products[k, 0][:], in1=products[k, 1][:], op=ALU.add)
+            engine = nc.vector if k == BANKS - 1 else nc.gpsimd
+            engine.tensor_tensor(out=rotated[k][:], in0=products[k, 0][:], in1=products[k, 1][:], op=ALU.add)
 
         def sum_squares(k):
             sums = stage.tile([P, BLOCK_HEADS], F32)
@@ -191,13 +197,29 @@ def tile_selfattention_pa_kernel(tc, x, freqs, w_words, w_scales, b, g, out):
 
         def scale_and_store(k):
             j, t = divmod(k, TOKEN_TILES)
-            result = stage.tile([P, N_BLOCK], F32)
+            result = results.tile([P, N_BLOCK], F32)
             for h in range(BLOCK_HEADS):
                 head = slice(h * HEAD, (h + 1) * HEAD)
                 nc.scalar.activation(
                     out=result[:, head], in_=rotated[k][:, head], func=ACT.Copy, scale=inv_rms[k][:, h : h + 1]
                 )
             nc.sync.dma_start(out=out_tiles[t][:, j * N_BLOCK : (j + 1) * N_BLOCK], in_=result[:])
+
+        def build_table(t):
+            gain = gain_bank[:, 0:HEAD].rearrange("p (j c) -> p c j", c=2).unsqueeze(3)
+            nc.vector.tensor_tensor(
+                out=tables_sb[:, t],
+                in0=freqs_sb[:, t, :].rearrange("p (j i c) -> p c j i", i=2, c=2),
+                in1=gain.to_broadcast([P, 2, PAIRS, 2]),
+                op=ALU.mult,
+            )
+            nc.tensor.matmul(
+                out=tables[t // 2][:, t % 2, :],
+                lhsT=identity[:],
+                rhs=tables_sb[:, t].rearrange("p c j i -> p (c j i)"),
+                start=True,
+                stop=True,
+            )
 
         nc.vector.memset(vectors[:], 0.0)
         nc.vector.memset(eps[:], EPS)
@@ -206,51 +228,30 @@ def tile_selfattention_pa_kernel(tc, x, freqs, w_words, w_scales, b, g, out):
         make_identity(nc, identity_bf[:])
         make_identity(nc, identity[:])
 
-        nc.scalar.dma_start(out=vectors[0:N_BLOCKS, :], in_=b.rearrange("(r n) -> r n", n=N_BLOCK))
-        nc.scalar.dma_start(out=vectors[N_BLOCKS : N_BLOCKS + 1, 0:HEAD], in_=g.rearrange("(r n) -> r n", n=HEAD))
-        nc.scalar.dma_start(out=freqs_sb[:], in_=freqs_rows)
-        for t in range(AHEAD):
+        load_tokens(0)
+        nc.sync.dma_start(out=vectors[0:N_BLOCKS, :], in_=b.rearrange("(r n) -> r n", n=N_BLOCK))
+        nc.sync.dma_start(out=vectors[N_BLOCKS : N_BLOCKS + 1, 0:HEAD], in_=g.rearrange("(r n) -> r n", n=HEAD))
+        nc.sync.dma_start(out=freqs_sb[:], in_=freqs_rows)
+        for t in range(1, TOKEN_TILES):
             load_tokens(t)
-        load_features(0)
-        for t in range(AHEAD, TOKEN_TILES):
-            load_tokens(t)
-        for j in range(1, N_BLOCKS):
+        for j in range(N_BLOCKS):
             load_features(j)
 
         nc.scalar.activation(out=warm[:], in_=eps[:], func=ACT.Abs_reciprocal_sqrt)
 
-        gain_bank = spread(N_BLOCKS)
-        for j in range(N_BLOCKS):
-            nc.scalar.copy(out=bias[j][:], in_=spread(j)[:])
-
-        sort_words(0)
-        gain = gain_bank[:, 0:HEAD].rearrange("p (j c) -> p c j", c=2).unsqueeze(3).to_broadcast([P, 2, PAIRS, 2])
         for t in range(TOKEN_TILES):
-            nc.vector.tensor_tensor(
-                out=tables_sb[:, t],
-                in0=freqs_sb[:, t, :].rearrange("p (j i c) -> p c j i", i=2, c=2),
-                in1=gain,
-                op=ALU.mult,
-            )
-        sort_words(1)
-        transpose_and_quantise(0)
+            transpose(t)
+            if t == 0:
+                spread(N_BLOCKS, gain_bank)
+                for j in range(N_BLOCKS):
+                    spread_bias(j)
+            build_table(t)
         for t in range(TOKEN_TILES):
-            nc.tensor.matmul(
-                out=tables[t // 2][:, t % 2, :],
-                lhsT=identity[:],
-                rhs=tables_sb[:, t].rearrange("p c j i -> p (c j i)"),
-                start=True,
-                stop=True,
-            )
-        transpose_and_quantise(1)
+            quantise(t)
 
         for k in range(BANKS + 2):
-            prepare = k + AHEAD < TOKEN_TILES
             if k < BANKS:
-                bank = project(k)
-                if prepare:
-                    sort_words(k + AHEAD)
-                add_bias(k, bank)
+                add_bias(k, project(k))
             if 1 <= k <= BANKS:
                 multiply_table(k - 1, 1)
                 add_products(k - 1)
@@ -261,5 +262,3 @@ def tile_selfattention_pa_kernel(tc, x, freqs, w_words, w_scales, b, g, out):
                 scale_and_store(k - 2)
             if k < BANKS:
                 invert_rms(k, sums)
-                if prepare:
-                    transpose_and_quantise(k + AHEAD)

@@ -27,7 +27,7 @@ BLOCK_HEADS = N_BLOCK // HEAD
 N_BLOCKS = FEATURES // N_BLOCK
 TOKEN_TILES = TOKENS // P
 BANKS = N_BLOCKS * TOKEN_TILES
-PLANE_BLOCKS = 2
+PLANE_GROUPS = ((0,), (1,), (2, 3), (4, 5))
 
 FLOPS = 2 * TOKENS * FEATURES * FEATURES
 
@@ -61,8 +61,8 @@ def tile_selfattention_pa_kernel(tc, x, freqs, w_words, w_scales, b, g, out):
             keep.tile([P, PASSES, 2 * N_BLOCK], U8, name="w_codes%d" % j, align_bytes=64) for j in range(N_BLOCKS)
         ]
         w_planes = [
-            keep.tile([P, PASSES, PLANE_BLOCKS * N_BLOCK], U8, name="w_planes%d" % s, align_bytes=64)
-            for s in range(N_BLOCKS // PLANE_BLOCKS)
+            keep.tile([P, PASSES, len(group) * N_BLOCK], U8, name="w_planes%d" % s, align_bytes=64)
+            for s, group in enumerate(PLANE_GROUPS)
         ]
         vectors = keep.tile([P, N_BLOCK], BF16)
         bias = [keep.tile([P, N_BLOCK], F32, name="bias%d" % j) for j in range(N_BLOCKS)]
@@ -78,20 +78,24 @@ def tile_selfattention_pa_kernel(tc, x, freqs, w_words, w_scales, b, g, out):
         def load_tokens(t):
             nc.sync.dma_start(out=x_raw[t][:], in_=x_tiles[t])
 
-        def load_features(j):
-            if j % PLANE_BLOCKS == 0:
-                s = j // PLANE_BLOCKS
-                words = PLANE_BLOCKS * N_BLOCK // 4
-                for r in range(4):
-                    nc.sync.dma_start(
-                        out=w_planes[s][r:P:32, :, :].bitcast(I32),
-                        in_=w_scales_i32[:, r:16:4, s * words : (s + 1) * words].rearrange("c q w -> q c w"),
-                    )
+        def load_scales(s):
+            group = PLANE_GROUPS[s]
+            first = group[0] * N_BLOCK // 4
+            words = len(group) * N_BLOCK // 4
+            for r in range(4):
+                nc.sync.dma_start(
+                    out=w_planes[s][r:P:32, :, :].bitcast(I32),
+                    in_=w_scales_i32[:, r:16:4, first : first + words].rearrange("c q w -> q c w"),
+                )
+
+        def load_words(j, pieces):
             words = 2 * N_BLOCK // 4
-            nc.sync.dma_start(
-                out=w_codes[j][:].bitcast(I32),
-                in_=w_words_i32[:, :, j * words : (j + 1) * words].rearrange("c p w -> p c w"),
-            )
+            step = PASSES // pieces
+            for c in range(0, PASSES, step):
+                nc.sync.dma_start(
+                    out=w_codes[j][:, c : c + step, :].bitcast(I32),
+                    in_=w_words_i32[c : c + step, :, j * words : (j + 1) * words].rearrange("c p w -> p c w"),
+                )
 
         def spread(row, bank):
             nc.tensor.matmul(
@@ -136,8 +140,10 @@ def tile_selfattention_pa_kernel(tc, x, freqs, w_words, w_scales, b, g, out):
         def project(k):
             j, t = divmod(k, TOKEN_TILES)
             bank = banks.tile([P, N_BLOCK], F32, tag="bank")
-            plane = w_planes[j // PLANE_BLOCKS]
-            cols = slice((j % PLANE_BLOCKS) * N_BLOCK, (j % PLANE_BLOCKS + 1) * N_BLOCK)
+            s = [j in group for group in PLANE_GROUPS].index(True)
+            plane = w_planes[s]
+            first = PLANE_GROUPS[s].index(j) * N_BLOCK
+            cols = slice(first, first + N_BLOCK)
             for c in range(PASSES):
                 nc.tensor.matmul_mx(
                     out=bank[:],
@@ -234,8 +240,10 @@ def tile_selfattention_pa_kernel(tc, x, freqs, w_words, w_scales, b, g, out):
         nc.sync.dma_start(out=freqs_sb[:], in_=freqs_rows)
         for t in range(1, TOKEN_TILES):
             load_tokens(t)
-        for j in range(N_BLOCKS):
-            load_features(j)
+        for s, group in enumerate(PLANE_GROUPS):
+            load_scales(s)
+            for j in group:
+                load_words(j, 2 if j == 0 else 1)
 
         nc.scalar.activation(out=warm[:], in_=eps[:], func=ACT.Abs_reciprocal_sqrt)
 

@@ -35,9 +35,9 @@ FLOPS = 2 * TOKENS * FEATURES * FEATURES
 def tile_selfattention_pa_kernel(tc, x, freqs, w_words, w_scales, b, g, out):
     nc = tc.nc
 
-    x_tiles = x.flatten_outer_dims().rearrange("(t p) k -> t p k", p=P)
-    out_tiles = out.flatten_outer_dims().rearrange("(t p h) d -> t p (h d)", p=P, h=FEATURES // HEAD)
-    freqs_rows = freqs.flatten_outer_dims().rearrange("(t p j i) c -> p t (j i c)", p=P, j=PAIRS, i=2)
+    x_tiles = x.flatten_outer_dims().rearrange("(p t) k -> t p k", p=P)
+    out_tiles = out.flatten_outer_dims().rearrange("(p t h) d -> t p (h d)", p=P, h=FEATURES // HEAD)
+    freqs_rows = freqs.flatten_outer_dims().rearrange("(p t j i) c -> p t (j i c)", p=P, j=PAIRS, i=2)
     w_words_i32 = w_words.bitcast(I32)
     w_scales_i32 = w_scales.bitcast(I32)
 
@@ -49,7 +49,8 @@ def tile_selfattention_pa_kernel(tc, x, freqs, w_words, w_scales, b, g, out):
         banks = ctx.enter_context(tc.psum_pool(name="banks", bufs=5))
         ctx.enter_context(tc.manual_schedule())
 
-        x_raw = [keep.tile([P, FEATURES], BF16, name="x_raw%d" % t) for t in range(TOKEN_TILES)]
+        x_first = [keep.tile([P, 2 * K_PASS], BF16, name="x_first%d" % h) for h in range(PASSES // 2)]
+        x_raw = [None] + [keep.tile([P, FEATURES], BF16, name="x_raw%d" % t) for t in range(1, TOKEN_TILES)]
         x_sorted = [keep.tile([P, PASSES, 2, P], F32, name="x_sorted%d" % t) for t in range(TOKEN_TILES)]
         x_codes = [
             keep.tile([P, PASSES, P], U32, name="x_codes%d" % t, align_bytes=64) for t in range(TOKEN_TILES)
@@ -58,7 +59,11 @@ def tile_selfattention_pa_kernel(tc, x, freqs, w_words, w_scales, b, g, out):
             keep.tile([P, PASSES, P], U8, name="x_planes%d" % t, align_bytes=64) for t in range(TOKEN_TILES)
         ]
         w_codes = [
-            keep.tile([P, PASSES, 2 * N_BLOCK], U8, name="w_codes%d" % j, align_bytes=64) for j in range(N_BLOCKS)
+            [
+                keep.tile([P, PASSES // pieces, 2 * N_BLOCK], U8, name="w_codes%d_%d" % (j, n), align_bytes=64)
+                for n in range(pieces)
+            ]
+            for j, pieces in enumerate((3, 1, 1, 1, 1, 1))
         ]
         w_planes = [
             keep.tile([P, PASSES, len(group) * N_BLOCK], U8, name="w_planes%d" % s, align_bytes=64)
@@ -76,7 +81,11 @@ def tile_selfattention_pa_kernel(tc, x, freqs, w_words, w_scales, b, g, out):
         gain_bank = table_banks.tile([P, N_BLOCK], F32)
 
         def load_tokens(t):
-            nc.sync.dma_start(out=x_raw[t][:], in_=x_tiles[t])
+            if t == 0:
+                for h, piece in enumerate(x_first):
+                    nc.sync.dma_start(out=piece[:], in_=x_tiles[0][:, h * 2 * K_PASS : (h + 1) * 2 * K_PASS])
+            else:
+                nc.sync.dma_start(out=x_raw[t][:], in_=x_tiles[t])
 
         def load_scales(s):
             group = PLANE_GROUPS[s]
@@ -88,13 +97,15 @@ def tile_selfattention_pa_kernel(tc, x, freqs, w_words, w_scales, b, g, out):
                     in_=w_scales_i32[:, r:16:4, first : first + words].rearrange("c q w -> q c w"),
                 )
 
-        def load_words(j, pieces):
+        def load_words(j):
             words = 2 * N_BLOCK // 4
-            step = PASSES // pieces
-            for c in range(0, PASSES, step):
+            step = PASSES // len(w_codes[j])
+            for n, piece in enumerate(w_codes[j]):
                 nc.sync.dma_start(
-                    out=w_codes[j][:, c : c + step, :].bitcast(I32),
-                    in_=w_words_i32[c : c + step, :, j * words : (j + 1) * words].rearrange("c p w -> p c w"),
+                    out=piece[:].bitcast(I32),
+                    in_=w_words_i32[n * step : (n + 1) * step, :, j * words : (j + 1) * words].rearrange(
+                        "c p w -> p c w"
+                    ),
                 )
 
         def spread(row, bank):
@@ -114,10 +125,11 @@ def tile_selfattention_pa_kernel(tc, x, freqs, w_words, w_scales, b, g, out):
         grouped = {}
 
         def transpose(t):
-            words = x_raw[t][:].bitcast(F32).rearrange("p (c r u) -> p c u r", r=P, u=2)
             for half in range(PASSES // 2):
                 passes = slice(2 * half, 2 * half + 2)
-                nc.vector.tensor_copy(out=x_sorted[t][:, passes], in_=words[:, passes])
+                piece = x_first[half][:] if t == 0 else x_raw[t][:, half * 2 * K_PASS : (half + 1) * 2 * K_PASS]
+                words = piece.bitcast(F32).rearrange("p (c r u) -> p c u r", r=P, u=2)
+                nc.vector.tensor_copy(out=x_sorted[t][:, passes], in_=words)
                 turned = banks.tile([P, 2, 2, P], F32, tag="bank")
                 for a in range(2):
                     for u in range(2):
@@ -144,12 +156,13 @@ def tile_selfattention_pa_kernel(tc, x, freqs, w_words, w_scales, b, g, out):
             plane = w_planes[s]
             first = PLANE_GROUPS[s].index(j) * N_BLOCK
             cols = slice(first, first + N_BLOCK)
+            step = PASSES // len(w_codes[j])
             for c in range(PASSES):
                 nc.tensor.matmul_mx(
                     out=bank[:],
                     lhsT=x_codes[t][:, c, :].bitcast(FP8X4),
                     lhsT_scale=x_planes[t][:, c, :],
-                    rhs=w_codes[j][:, c, :].bitcast(FP4X4),
+                    rhs=w_codes[j][c // step][:, c % step, :].bitcast(FP4X4),
                     rhs_scale=plane[:, c, cols],
                     start=(c == 0),
                     stop=(c == PASSES - 1),
@@ -243,7 +256,7 @@ def tile_selfattention_pa_kernel(tc, x, freqs, w_words, w_scales, b, g, out):
         for s, group in enumerate(PLANE_GROUPS):
             load_scales(s)
             for j in group:
-                load_words(j, 2 if j == 0 else 1)
+                load_words(j)
 
         nc.scalar.activation(out=warm[:], in_=eps[:], func=ACT.Abs_reciprocal_sqrt)
 

@@ -43,8 +43,8 @@ def tile_selfattention_pa_kernel(tc, x, freqs, w_words, w_scales, b, g, out):
 
     with ExitStack() as ctx:
         keep = ctx.enter_context(tc.tile_pool(name="keep", bufs=1))
-        stage = ctx.enter_context(tc.tile_pool(name="stage", bufs=4))
-        results = ctx.enter_context(tc.tile_pool(name="results", bufs=8))
+        stage = ctx.enter_context(tc.tile_pool(name="stage", bufs=6))
+        results = ctx.enter_context(tc.tile_pool(name="results", bufs=12))
         table_banks = ctx.enter_context(tc.psum_pool(name="table_banks", bufs=1))
         banks = ctx.enter_context(tc.psum_pool(name="banks", bufs=5))
         ctx.enter_context(tc.manual_schedule())

from contextlib import ExitStack

import concourse.mybir as mybir
from concourse.masks import make_identity

F32 = mybir.dt.float32
BF16 = mybir.dt.bfloat16
I32 = mybir.dt.int32
U32 = mybir.dt.uint32
U8 = mybir.dt.uint8
FP8X4 = mybir.dt.float8_e4m3fn_x4
FP4X4 = mybir.dt.float4_e2m1fn_x4
ACT = mybir.ActivationFunctionType
ALU = mybir.AluOpType

P = 128
TOKENS = 512
FEATURES = 3072
HEAD = 128
PAIRS = HEAD // 2
EPS = 1e-6

K_PASS = 4 * P
PASSES = FEATURES // K_PASS
N_BLOCK = 512
BLOCK_HEADS = N_BLOCK // HEAD
N_BLOCKS = FEATURES // N_BLOCK
TOKEN_TILES = TOKENS // P
BANKS = N_BLOCKS * TOKEN_TILES
PLANE_GROUPS = ((0,), (1,), (2, 3), (4, 5))

FLOPS = 2 * TOKENS * FEATURES * FEATURES


def tile_selfattention_pa_kernel(tc, x, freqs, w_words, w_scales, b, g, out):
    nc = tc.nc

    x_tiles = x.flatten_outer_dims().rearrange("(p t) k -> t p k", p=P)
    out_tiles = out.flatten_outer_dims().rearrange("(p t h) d -> t p (h d)", p=P, h=FEATURES // HEAD)
    freqs_rows = freqs.flatten_outer_dims().rearrange("(p t j i) c -> p t (j i c)", p=P, j=PAIRS, i=2)
    w_words_i32 = w_words.bitcast(I32)
    w_scales_i32 = w_scales.bitcast(I32)

    with ExitStack() as ctx:
        keep = ctx.enter_context(tc.tile_pool(name="keep", bufs=1))
        stage = ctx.enter_context(tc.tile_pool(name="stage", bufs=6))
        results = ctx.enter_context(tc.tile_pool(name="results", bufs=12))
        table_banks = ctx.enter_context(tc.psum_pool(name="table_banks", bufs=1))
        banks = ctx.enter_context(tc.psum_pool(name="banks", bufs=5))
        ctx.enter_context(tc.manual_schedule())

        x_first = [keep.tile([P, 2 * K_PASS], BF16, name="x_first%d" % h) for h in range(PASSES // 2)]
        x_raw = [None] + [keep.tile([P, FEATURES], BF16, name="x_raw%d" % t) for t in range(1, TOKEN_TILES)]
        x_sorted = [keep.tile([P, PASSES, 2, P], F32, name="x_sorted%d" % t) for t in range(TOKEN_TILES)]
        x_codes = [
            keep.tile([P, PASSES, P], U32, name="x_codes%d" % t, align_bytes=64) for t in range(TOKEN_TILES)
        ]
        x_planes = [
            keep.tile([P, PASSES, P], U8, name="x_planes%d" % t, align_bytes=64) for t in range(TOKEN_TILES)
        ]
        w_codes = [
            [
                keep.tile([P, PASSES // pieces, 2 * N_BLOCK], U8, name="w_codes%d_%d" % (j, n), align_bytes=64)
                for n in range(pieces)
            ]
            for j, pieces in enumerate((3, 1, 1, 1, 1, 1))
        ]
        w_planes = [
            keep.tile([P, PASSES, len(group) * N_BLOCK], U8, name="w_planes%d" % s, align_bytes=64)
            for s, group in enumerate(PLANE_GROUPS)
        ]
        vectors = keep.tile([P, N_BLOCK], BF16)
        bias = [keep.tile([P, N_BLOCK], F32, name="bias%d" % j) for j in range(N_BLOCKS)]
        freqs_sb = keep.tile([P, TOKEN_TILES, 4 * PAIRS], BF16)
        tables_sb = keep.tile([P, TOKEN_TILES, 2, PAIRS, 2], F32)
        identity = keep.tile([P, P], F32)
        identity_bf = keep.tile([P, P], BF16)
        eps = keep.tile([P, 1], F32)
        warm = keep.tile([P, 1], F32)
        tables = [table_banks.tile([P, 2, 4 * PAIRS], F32, name="tables%d" % s) for s in range(TOKEN_TILES // 2)]
        gain_bank = table_banks.tile([P, N_BLOCK], F32)

        def load_tokens(t):
            if t == 0:
                for h, piece in enumerate(x_first):
                    nc.sync.dma_start(out=piece[:], in_=x_tiles[0][:, h * 2 * K_PASS : (h + 1) * 2 * K_PASS])
            else:
                nc.sync.dma_start(out=x_raw[t][:], in_=x_tiles[t])

        def load_scales(s):
            group = PLANE_GROUPS[s]
            first = group[0] * N_BLOCK // 4
            words = len(group) * N_BLOCK // 4
            for r in range(4):
                nc.sync.dma_start(
                    out=w_planes[s][r:P:32, :, :].bitcast(I32),
                    in_=w_scales_i32[:, r:16:4, first : first + words].rearrange("c q w -> q c w"),
                )

        def load_words(j):
            words = 2 * N_BLOCK // 4
            step = PASSES // len(w_codes[j])
            for n, piece in enumerate(w_codes[j]):
                nc.sync.dma_start(
                    out=piece[:].bitcast(I32),
                    in_=w_words_i32[n * step : (n + 1) * step, :, j * words : (j + 1) * words].rearrange(
                        "c p w -> p c w"
                    ),
                )

        def spread(row, bank):
            nc.tensor.matmul(
                out=bank[:],
                lhsT=identity_bf[:, row : row + 1].to_broadcast([P, P]),
                rhs=vectors[:],
                start=True,
                stop=True,
            )

        def spread_bias(j):
            bank = banks.tile([P, N_BLOCK], F32, tag="bank")
            spread(j, bank)
            nc.scalar.copy(out=bias[j][:], in_=bank[:])

        grouped = {}

        def transpose(t):
            for half in range(PASSES // 2):
                passes = slice(2 * half, 2 * half + 2)
                piece = x_first[half][:] if t == 0 else x_raw[t][:, half * 2 * K_PASS : (half + 1) * 2 * K_PASS]
                words = piece.bitcast(F32).rearrange("p (c r u) -> p c u r", r=P, u=2)
                nc.vector.tensor_copy(out=x_sorted[t][:, passes], in_=words)
                turned = banks.tile([P, 2, 2, P], F32, tag="bank")
                for a in range(2):
                    for u in range(2):
                        nc.tensor.transpose(turned[:, a, u, :], x_sorted[t][:, 2 * half + a, u, :], identity[:])
                grouped[t, half] = stage.tile([P, 2 * K_PASS], BF16, name="grouped", bufs=TOKEN_TILES * PASSES // 2, align_bytes=64)
                nc.scalar.copy(
                    out=grouped[t, half][:].bitcast(F32).rearrange("p (a r u) -> p a r u", a=2, u=2),
                    in_=turned[:].rearrange("p a u r -> p a r u"),
                )

        def quantise(t):
            for half in range(PASSES // 2):
                passes = slice(2 * half, 2 * half + 2)
                nc.vector.quantize_mx(
                    out=x_codes[t][:, passes, :].rearrange("p a r -> p (a r)").bitcast(FP8X4),
                    scales=x_planes[t][:, passes, :].rearrange("p a r -> p (a r)"),
                    in_=grouped[t, half][:],
                )

        def project(k):
            j, t = divmod(k, TOKEN_TILES)
            bank = banks.tile([P, N_BLOCK], F32, tag="bank")
            s = [j in group for group in PLANE_GROUPS].index(True)
            plane = w_planes[s]
            first = PLANE_GROUPS[s].index(j) * N_BLOCK
            cols = slice(first, first + N_BLOCK)
            step = PASSES // len(w_codes[j])
            for c in range(PASSES):
                nc.tensor.matmul_mx(
                    out=bank[:],
                    lhsT=x_codes[t][:, c, :].bitcast(FP8X4),
                    lhsT_scale=x_planes[t][:, c, :],
                    rhs=w_codes[j][c // step][:, c % step, :].bitcast(FP4X4),
                    rhs_scale=plane[:, c, cols],
                    start=(c == 0),
                    stop=(c == PASSES - 1),
                )
            return bank

        biased = {}
        products = {}
        rotated = {}
        inv_rms = {}

        def add_bias(k, bank):
            biased[k] = stage.tile([P, N_BLOCK], F32, name="biased")
            nc.vector.tensor_tensor(out=biased[k][:], in0=bank[:], in1=bias[k // TOKEN_TILES][:], op=ALU.add)

        def multiply_table(k, c):
            t = k % TOKEN_TILES
            shape = [P, BLOCK_HEADS, PAIRS, 2]
            table = tables[t // 2][:, t % 2, :].rearrange("p (c j i) -> p c j i", c=2, i=2)
            pairs = biased[k][:].rearrange("p (h j c) -> p h j c", h=BLOCK_HEADS, c=2)
            products[k, c] = stage.tile([P, N_BLOCK], F32, name="product%d" % c)
            nc.vector.tensor_tensor(
                out=products[k, c][:].rearrange("p (h j i) -> p h j i", h=BLOCK_HEADS, i=2),
                in0=pairs[:, :, :, c : c + 1].to_broadcast(shape),
                in1=table[:, c].unsqueeze(1).to_broadcast(shape),
                op=ALU.mult,
            )

        def add_products(k):
            rotated[k] = stage.tile([P, N_BLOCK], F32, name="rotated")
            engine = nc.vector if k == BANKS - 1 else nc.gpsimd
            engine.tensor_tensor(out=rotated[k][:], in0=products[k, 0][:], in1=products[k, 1][:], op=ALU.add)

        def sum_squares(k):
            sums = stage.tile([P, BLOCK_HEADS], F32)
            for h in range(BLOCK_HEADS):
                squares = stage.tile([P, HEAD], F32)
                nc.scalar.activation(
                    out=squares[:],
                    in_=biased[k][:, h * HEAD : (h + 1) * HEAD],
                    func=ACT.Square,
                    accum_out=sums[:, h : h + 1],
                )
            return sums

        def invert_rms(k, sums):
            inv_rms[k] = stage.tile([P, BLOCK_HEADS], F32, name="inv_rms")
            nc.scalar.activation(
                out=inv_rms[k][:], in_=sums[:], func=ACT.Abs_reciprocal_sqrt, bias=eps[:], scale=1.0 / HEAD
            )

        def scale_and_store(k):
            j, t = divmod(k, TOKEN_TILES)
            result = results.tile([P, N_BLOCK], F32)
            for h in range(BLOCK_HEADS):
                head = slice(h * HEAD, (h + 1) * HEAD)
                nc.scalar.activation(
                    out=result[:, head], in_=rotated[k][:, head], func=ACT.Copy, scale=inv_rms[k][:, h : h + 1]
                )
            nc.sync.dma_start(out=out_tiles[t][:, j * N_BLOCK : (j + 1) * N_BLOCK], in_=result[:])

        def build_table(t):
            gain = gain_bank[:, 0:HEAD].rearrange("p (j c) -> p c j", c=2).unsqueeze(3)
            nc.vector.tensor_tensor(
                out=tables_sb[:, t],
                in0=freqs_sb[:, t, :].rearrange("p (j i c) -> p c j i", i=2, c=2),
                in1=gain.to_broadcast([P, 2, PAIRS, 2]),
                op=ALU.mult,
            )
            nc.tensor.matmul(
                out=tables[t // 2][:, t % 2, :],
                lhsT=identity[:],
                rhs=tables_sb[:, t].rearrange("p c j i -> p (c j i)"),
                start=True,
                stop=True,
            )

        nc.vector.memset(vectors[:], 0.0)
        nc.vector.memset(eps[:], EPS)
        for plane in w_planes:
            nc.vector.memset(plane[:].bitcast(I32), 0)
        make_identity(nc, identity_bf[:])
        make_identity(nc, identity[:])

        load_tokens(0)
        nc.sync.dma_start(out=vectors[0:N_BLOCKS, :], in_=b.rearrange("(r n) -> r n", n=N_BLOCK))
        nc.sync.dma_start(out=vectors[N_BLOCKS : N_BLOCKS + 1, 0:HEAD], in_=g.rearrange("(r n) -> r n", n=HEAD))
        nc.sync.dma_start(out=freqs_sb[:], in_=freqs_rows)
        for t in range(1, TOKEN_TILES):
            load_tokens(t)
        for s, group in enumerate(PLANE_GROUPS):
            load_scales(s)
            for j in group:
                load_words(j)

        nc.scalar.activation(out=warm[:], in_=eps[:], func=ACT.Abs_reciprocal_sqrt)

        for t in range(TOKEN_TILES):
            transpose(t)
            if t == 0:
                spread(N_BLOCKS, gain_bank)
                for j in range(N_BLOCKS):
                    spread_bias(j)
            build_table(t)
        for t in range(TOKEN_TILES):
            quantise(t)

        for k in range(BANKS + 2):
            if k < BANKS:
                add_bias(k, project(k))
            if 1 <= k <= BANKS:
                multiply_table(k - 1, 1)
                add_products(k - 1)
            if k < BANKS:
                multiply_table(k, 0)
                sums = sum_squares(k)
            if k >= 2:
                scale_and_store(k - 2)
            if k < BANKS:
                invert_rms(k, sums)
